import numpy as np
import ml_dtypes


def mxq(x, axis, fmt="e4m3"):
    dtype, down = {"e4m3": (ml_dtypes.float8_e4m3fn, 7), "e5m2": (ml_dtypes.float8_e5m2, 14)}[fmt]
    v = np.moveaxis(np.asarray(x, np.float32).astype(ml_dtypes.bfloat16).astype(np.float64), axis, -1)
    blocks = v.reshape(v.shape[:-1] + (-1, 32))
    amax = np.abs(blocks).max(-1, keepdims=True)
    byte = np.maximum(np.where(amax > 0, np.frexp(amax)[1] - 1 + 127, 0) - down, 1)
    scale = np.exp2(byte - 127.0)
    codes = (blocks / scale).astype(np.float32).astype(dtype).astype(np.float64)
    return np.moveaxis((codes * scale).reshape(v.shape), -1, axis)


WIDE = False


def mx_kscale(k):
    if not WIDE:
        return np.ones(k)
    levels = np.array([30, -30])
    if k % 512:
        return np.exp2(np.random.permutation(np.resize(levels, k // 32))).repeat(32)
    a = np.empty((k // 512, 16))
    for p in range(k // 512):
        a[p, :8] = np.random.permutation(np.resize(levels, 8))
        for g in range(8):
            far = levels[np.abs(levels - a[p, g]) >= 10]
            a[p, g + 8] = far[np.random.randint(len(far))]
    return np.exp2(a.ravel()).repeat(32)


BF16 = ml_dtypes.bfloat16


def bf(x):
    return np.asarray(x, np.float32).astype(BF16)


def f64(x):
    return np.asarray(x).astype(np.float64)


B, N, D, F, C, L = 1024, 4096, 1024, 1024, 128, 28
EPS = 1e-12


def l2norm(x):
    n = np.sqrt(np.sum(x * x, axis=1, keepdims=True))
    return x / np.maximum(n, EPS)


def setup_inputs():
    s = mx_kscale(D)
    return {"features": bf(np.random.standard_normal((B, D)) * s),
            "ex_features": bf(np.random.standard_normal((N, D)) * s),
            "g_weight": bf(np.random.standard_normal((F, D)) / np.sqrt(D) / s)}


def reference(features, ex_features, g_weight):
    gq = mxq(f64(g_weight), 1, "e4m3")
    f = mxq(f64(features), 1, "e5m2") @ gq.T
    exf = mxq(f64(ex_features), 1, "e5m2") @ gq.T
    return l2norm(f), l2norm(exf)

@@ -1,0 +1,194 @@
+from contextlib import ExitStack
+
+import concourse.mybir as mybir
+from concourse.masks import make_identity
+
+B, N, D, F = 1024, 4096, 1024, 1024
+EPS = 1e-12
+FLOPS = 2 * (B + N) * D * F
+
+F32 = mybir.dt.float32
+BF16 = mybir.dt.bfloat16
+U32 = mybir.dt.uint32
+U8 = mybir.dt.uint8
+E4M3 = mybir.dt.float8_e4m3fn_x4
+E5M2 = mybir.dt.float8_e5m2_x4
+ALU = mybir.AluOpType
+ACT = mybir.ActivationFunctionType
+
+P = 128
+PASSES = D // 512
+PASS_WORDS = 256
+BANK = 512
+HALVES = F // BANK
+BANKS = 8
+RUN = 4
+FIRST_RUNS = [1, 1, 2]
+LAG = 2
+VECTOR_COPY_EVERY = 4
+RESULT_BUFS = 16
+
+
+def tile_minerva_old_pa_kernel(tc, features, ex_features, g_weight, out_0, out_1):
+    nc = tc.nc
+
+    runs = []
+    sizes = FIRST_RUNS + [RUN] * ((B // P - sum(FIRST_RUNS)) // RUN)
+    row = 0
+    for size in sizes:
+        runs.append((features, out_0, row, size))
+        row += size * P
+    for row in range(0, N, RUN * P):
+        runs.append((ex_features, out_1, row, RUN))
+
+    with ExitStack() as ctx:
+        keep = ctx.enter_context(tc.tile_pool(name="keep", bufs=1))
+        stage = ctx.enter_context(tc.tile_pool(name="stage", bufs=2 * RUN))
+        small = ctx.enter_context(tc.tile_pool(name="small", bufs=2 * RUN))
+        results = ctx.enter_context(tc.tile_pool(name="results", bufs=RESULT_BUFS))
+        scratch = ctx.enter_context(tc.tile_pool(name="scratch", bufs=2))
+        psum = ctx.enter_context(tc.psum_pool(name="psum", bufs=1))
+        ctx.enter_context(tc.manual_schedule())
+
+        ident = keep.tile([P, P], F32)
+        make_identity(nc, ident[:])
+        minus_half = keep.tile([P, 1], F32)
+        nc.gpsimd.memset(minus_half[:], -0.5)
+
+        w_codes = keep.tile([P, PASSES, F], U32, align_bytes=64)
+        w_scales = keep.tile([P, PASSES, F], U8, align_bytes=64)
+
+        banks_taken = []
+
+        def take_bank():
+            number = len(banks_taken) % BANKS
+            bank = psum.tile([P, BANK], F32, name="bank%d" % number, tag="bank%d" % number)
+            banks_taken.append(number)
+            return bank
+
+        def load_weight(j):
+            rows = keep.tile([P, D], BF16, name="w_rows%d" % j, tag="w_rows%d" % j)
+            nc.sync.dma_start(out=rows[:], in_=g_weight[j * P : (j + 1) * P, :])
+            return rows[:]
+
+        def load_run(j):
+            source, dest, row0, size = runs[j]
+            rows = keep.tile([P, size, D], BF16, name="x_rows%d" % j, tag="x_rows%d" % j)
+            nc.sync.dma_start(out=rows[:], in_=source[row0 : row0 + size * P, :].rearrange("(p t) k -> p t k", t=size))
+            return [rows[:, t, :] for t in range(size)]
+
+        def transpose(rows):
+            words = rows.bitcast(F32)
+            bank = take_bank()
+            for g in range(PASSES):
+                for u in range(2):
+                    col = (2 * g + u) * P
+                    nc.tensor.transpose(
+                        bank[:, col : col + P], words[:, PASS_WORDS * g + u : PASS_WORDS * (g + 1) : 2], ident[:]
+                    )
+            return bank
+
+        def copy_out(bank, on_vector):
+            grouped = stage.tile([P, BANK], F32, name="grouped", tag="grouped", align_bytes=64)
+            dst = grouped[:].rearrange("p (g r u) -> p g r u", g=PASSES, u=2)
+            src = bank[:].rearrange("p (g u r) -> p g r u", g=PASSES, u=2)
+            if on_vector:
+                nc.vector.tensor_copy(out=dst, in_=src)
+            else:
+                nc.scalar.copy(out=dst, in_=src)
+            return grouped
+
+        def quantize_weight(j, grouped):
+            for g in range(PASSES):
+                cols = slice(j * P, (j + 1) * P)
+                nc.vector.quantize_mx(
+                    out=w_codes[:, g, cols].bitcast(E4M3),
+                    scales=w_scales[:, g, cols],
+                    in_=grouped[:, PASS_WORDS * g : PASS_WORDS * (g + 1)].bitcast(BF16),
+                )
+
+        def quantize_rows(grouped):
+            x_codes = stage.tile([P, PASSES * P], U32, name="x_codes", tag="x_codes", align_bytes=64)
+            x_scales = stage.tile([P, PASSES * P], U8, name="x_scales", tag="x_scales", align_bytes=64)
+            nc.vector.quantize_mx(out=x_codes[:].bitcast(E5M2), scales=x_scales[:], in_=grouped[:].bitcast(BF16))
+            return x_codes, x_scales
+
+        def multiply(x_codes, x_scales):
+            sums = small.tile([P, HALVES], F32, name="sums", tag="sums")
+            banks = []
+            for h in range(HALVES):
+                bank = take_bank()
+                cols = slice(h * BANK, (h + 1) * BANK)
+                for g in range(PASSES):
+                    nc.tensor.matmul_mx(
+                        out=bank[:],
+                        lhsT=x_codes[:, g * P : (g + 1) * P].bitcast(E5M2),
+                        lhsT_scale=x_scales[:, g * P : (g + 1) * P],
+                        rhs=w_codes[:, g, cols].bitcast(E4M3),
+                        rhs_scale=w_scales[:, g, cols],
+                        start=(g == 0),
+                        stop=(g == PASSES - 1),
+                    )
+                squares = scratch.tile([P, BANK], F32, name="squares", tag="squares")
+                nc.scalar.activation(out=squares[:], in_=bank[:], func=ACT.Square, accum_out=sums[:, h : h + 1])
+                banks.append(bank)
+            floored = small.tile([P, 1], F32, name="floored", tag="floored")
+            nc.gpsimd.tensor_scalar(
+                out=floored[:], in0=sums[:, 0:1], scalar1=sums[:, 1:2], scalar2=EPS * EPS, op0=ALU.add, op1=ALU.max
+            )
+            inverse = small.tile([P, 1], F32, name="inverse", tag="inverse")
+            nc.gpsimd.tensor_tensor(out=inverse[:], in0=floored[:], in1=minus_half[:], op=ALU.pow)
+            return banks, inverse
+
+        def scale_and_store(banks, inverse, dest_rows):
+            result = results.tile([P, F], F32, name="result", tag="result")
+            for h in range(HALVES):
+                nc.vector.tensor_scalar(
+                    out=result[:, h * BANK : (h + 1) * BANK],
+                    in0=banks[h][:],
+                    scalar1=inverse[:],
+                    scalar2=None,
+                    op0=ALU.mult,
+                )
+            nc.sync.dma_start(out=dest_rows, in_=result[:])
+
+        def scale_and_store_last(banks, inverse, dest_rows):
+            result = results.tile([P, F], F32, name="result", tag="result")
+            nc.vector.tensor_scalar(
+                out=result[:, :BANK], in0=banks[0][:], scalar1=inverse[:], scalar2=None, op0=ALU.mult
+            )
+            nc.scalar.activation(out=result[:, BANK:], in_=banks[1][:], func=ACT.Copy, scale=inverse[:])
+            nc.sync.dma_start(out=dest_rows, in_=result[:])
+
+        w_tiles = F // P
+        w_rows = [load_weight(j) for j in range(w_tiles // 2)]
+        x_rows = [load_run(0)]
+        w_rows += [load_weight(j) for j in range(w_tiles // 2, w_tiles)]
+        x_rows += [load_run(j) for j in range(1, len(runs))]
+
+        quantized = []
+        for j in range(w_tiles):
+            quantize_weight(j, copy_out(transpose(w_rows[j]), j % VECTOR_COPY_EVERY == 1))
+            if j == w_tiles // 2 - 1:
+                quantized = [quantize_rows(copy_out(transpose(rows), False)) for rows in x_rows[0]]
+
+        waiting = []
+        for j, (source, dest, row0, size) in enumerate(runs):
+            ahead = x_rows[j + 1] if j + 1 < len(runs) else []
+            turned = [transpose(rows) for rows in ahead]
+            for item in waiting:
+                scale_and_store(*item)
+            waiting = []
+            grouped = [copy_out(bank, t == VECTOR_COPY_EVERY - 1) for t, bank in enumerate(turned)]
+            quantized_ahead = [quantize_rows(tile) for tile in grouped]
+            dest_tiles = dest[row0 : row0 + size * P, :].rearrange("(p t) f -> p t f", t=size)
+            for t in range(size):
+                banks, inverse = multiply(*quantized[t])
+                if t < size - LAG:
+                    scale_and_store(banks, inverse, dest_tiles[:, t, :])
+                else:
+                    waiting.append((banks, inverse, dest_tiles[:, t, :]))
+            quantized = quantized_ahead
+        for item in waiting[:-1]:
+            scale_and_store(*item)
+        scale_and_store_last(*waiting[-1])

@@ -22,29 +22,21 @@ PASS_WORDS = 256
 BANK = 512
 HALVES = F // BANK
 BANKS = 8
-RUN = 4
-FIRST_RUNS = [1, 1, 2]
-LAG = 2
-VECTOR_COPY_EVERY = 4
+RUN = 2
+VECTOR_COPY_EVERY = 3
 RESULT_BUFS = 16
 
 
 def tile_minerva_old_pa_kernel(tc, features, ex_features, g_weight, out_0, out_1):
     nc = tc.nc
 
-    runs = []
-    sizes = FIRST_RUNS + [RUN] * ((B // P - sum(FIRST_RUNS)) // RUN)
-    row = 0
-    for size in sizes:
-        runs.append((features, out_0, row, size))
-        row += size * P
-    for row in range(0, N, RUN * P):
-        runs.append((ex_features, out_1, row, RUN))
+    runs = [(features, out_0, row) for row in range(0, B, RUN * P)]
+    runs += [(ex_features, out_1, row) for row in range(0, N, RUN * P)]
 
     with ExitStack() as ctx:
         keep = ctx.enter_context(tc.tile_pool(name="keep", bufs=1))
-        stage = ctx.enter_context(tc.tile_pool(name="stage", bufs=2 * RUN))
-        small = ctx.enter_context(tc.tile_pool(name="small", bufs=2 * RUN))
+        stage = ctx.enter_context(tc.tile_pool(name="stage", bufs=3 * RUN))
+        small = ctx.enter_context(tc.tile_pool(name="small", bufs=3 * RUN))
         results = ctx.enter_context(tc.tile_pool(name="results", bufs=RESULT_BUFS))
         scratch = ctx.enter_context(tc.tile_pool(name="scratch", bufs=2))
         psum = ctx.enter_context(tc.psum_pool(name="psum", bufs=1))
@@ -58,13 +50,13 @@ def tile_minerva_old_pa_kernel(tc, features, ex_features, g_weight, out_0, out_1
         w_codes = keep.tile([P, PASSES, F], U32, align_bytes=64)
         w_scales = keep.tile([P, PASSES, F], U8, align_bytes=64)
 
-        banks_taken = []
+        free_banks = list(range(BANKS))
 
         def take_bank():
-            number = len(banks_taken) % BANKS
+            number = free_banks[0]
+            free_banks.remove(number)
             bank = psum.tile([P, BANK], F32, name="bank%d" % number, tag="bank%d" % number)
-            banks_taken.append(number)
-            return bank
+            return number, bank
 
         def load_weight(j):
             rows = keep.tile([P, D], BF16, name="w_rows%d" % j, tag="w_rows%d" % j)
@@ -72,23 +64,24 @@ def tile_minerva_old_pa_kernel(tc, features, ex_features, g_weight, out_0, out_1
             return rows[:]
 
         def load_run(j):
-            source, dest, row0, size = runs[j]
-            rows = keep.tile([P, size, D], BF16, name="x_rows%d" % j, tag="x_rows%d" % j)
-            nc.sync.dma_start(out=rows[:], in_=source[row0 : row0 + size * P, :].rearrange("(p t) k -> p t k", t=size))
-            return [rows[:, t, :] for t in range(size)]
+            source, dest, row0 = runs[j]
+            rows = keep.tile([P, RUN, D], BF16, name="x_rows%d" % j, tag="x_rows%d" % j)
+            nc.sync.dma_start(out=rows[:], in_=source[row0 : row0 + RUN * P, :].rearrange("(p t) k -> p t k", t=RUN))
+            return [rows[:, t, :] for t in range(RUN)]
 
         def transpose(rows):
             words = rows.bitcast(F32)
-            bank = take_bank()
+            number, bank = take_bank()
             for g in range(PASSES):
                 for u in range(2):
                     col = (2 * g + u) * P
                     nc.tensor.transpose(
                         bank[:, col : col + P], words[:, PASS_WORDS * g + u : PASS_WORDS * (g + 1) : 2], ident[:]
                     )
-            return bank
+            return number, bank
 
-        def copy_out(bank, on_vector):
+        def copy_out(taken, on_vector):
+            number, bank = taken
             grouped = stage.tile([P, BANK], F32, name="grouped", tag="grouped", align_bytes=64)
             dst = grouped[:].rearrange("p (g r u) -> p g r u", g=PASSES, u=2)
             src = bank[:].rearrange("p (g u r) -> p g r u", g=PASSES, u=2)
@@ -96,6 +89,7 @@ def tile_minerva_old_pa_kernel(tc, features, ex_features, g_weight, out_0, out_1
                 nc.vector.tensor_copy(out=dst, in_=src)
             else:
                 nc.scalar.copy(out=dst, in_=src)
+            free_banks.append(number)
             return grouped
 
         def quantize_weight(j, grouped):
@@ -113,82 +107,108 @@ def tile_minerva_old_pa_kernel(tc, features, ex_features, g_weight, out_0, out_1
             nc.vector.quantize_mx(out=x_codes[:].bitcast(E5M2), scales=x_scales[:], in_=grouped[:].bitcast(BF16))
             return x_codes, x_scales
 
-        def multiply(x_codes, x_scales):
+        def multiply_half(operand, h, sums):
+            x_codes, x_scales = operand
+            number, bank = take_bank()
+            cols = slice(h * BANK, (h + 1) * BANK)
+            for g in range(PASSES):
+                nc.tensor.matmul_mx(
+                    out=bank[:],
+                    lhsT=x_codes[:, g * P : (g + 1) * P].bitcast(E5M2),
+                    lhsT_scale=x_scales[:, g * P : (g + 1) * P],
+                    rhs=w_codes[:, g, cols].bitcast(E4M3),
+                    rhs_scale=w_scales[:, g, cols],
+                    start=(g == 0),
+                    stop=(g == PASSES - 1),
+                )
+            squares = scratch.tile([P, BANK], F32, name="squares", tag="squares")
+            nc.scalar.activation(out=squares[:], in_=bank[:], func=ACT.Square, accum_out=sums[:, h : h + 1])
+            return number, bank
+
+        def new_sums():
             sums = small.tile([P, HALVES], F32, name="sums", tag="sums")
-            banks = []
-            for h in range(HALVES):
-                bank = take_bank()
-                cols = slice(h * BANK, (h + 1) * BANK)
-                for g in range(PASSES):
-                    nc.tensor.matmul_mx(
-                        out=bank[:],
-                        lhsT=x_codes[:, g * P : (g + 1) * P].bitcast(E5M2),
-                        lhsT_scale=x_scales[:, g * P : (g + 1) * P],
-                        rhs=w_codes[:, g, cols].bitcast(E4M3),
-                        rhs_scale=w_scales[:, g, cols],
-                        start=(g == 0),
-                        stop=(g == PASSES - 1),
-                    )
-                squares = scratch.tile([P, BANK], F32, name="squares", tag="squares")
-                nc.scalar.activation(out=squares[:], in_=bank[:], func=ACT.Square, accum_out=sums[:, h : h + 1])
-                banks.append(bank)
+            return sums
+
+        def inverse_norm(sums):
             floored = small.tile([P, 1], F32, name="floored", tag="floored")
             nc.gpsimd.tensor_scalar(
                 out=floored[:], in0=sums[:, 0:1], scalar1=sums[:, 1:2], scalar2=EPS * EPS, op0=ALU.add, op1=ALU.max
             )
             inverse = small.tile([P, 1], F32, name="inverse", tag="inverse")
             nc.gpsimd.tensor_tensor(out=inverse[:], in0=floored[:], in1=minus_half[:], op=ALU.pow)
-            return banks, inverse
+            return inverse
 
-        def scale_and_store(banks, inverse, dest_rows):
+        def new_result():
             result = results.tile([P, F], F32, name="result", tag="result")
-            for h in range(HALVES):
-                nc.vector.tensor_scalar(
-                    out=result[:, h * BANK : (h + 1) * BANK],
-                    in0=banks[h][:],
-                    scalar1=inverse[:],
-                    scalar2=None,
-                    op0=ALU.mult,
-                )
-            nc.sync.dma_start(out=dest_rows, in_=result[:])
+            return result
+
+        def scale_half(item, h, result):
+            banks, inverse, dest_rows = item
+            number, bank = banks[h]
+            nc.vector.tensor_scalar(
+                out=result[:, h * BANK : (h + 1) * BANK], in0=bank[:], scalar1=inverse[:], scalar2=None, op0=ALU.mult
+            )
+            free_banks.append(number)
+            if h == HALVES - 1:
+                nc.sync.dma_start(out=dest_rows, in_=result[:])
 
         def scale_and_store_last(banks, inverse, dest_rows):
             result = results.tile([P, F], F32, name="result", tag="result")
             nc.vector.tensor_scalar(
-                out=result[:, :BANK], in0=banks[0][:], scalar1=inverse[:], scalar2=None, op0=ALU.mult
+                out=result[:, :BANK], in0=banks[0][1][:], scalar1=inverse[:], scalar2=None, op0=ALU.mult
             )
-            nc.scalar.activation(out=result[:, BANK:], in_=banks[1][:], func=ACT.Copy, scale=inverse[:])
+            nc.scalar.activation(out=result[:, BANK:], in_=banks[1][1][:], func=ACT.Copy, scale=inverse[:])
             nc.sync.dma_start(out=dest_rows, in_=result[:])
 
+        def dest_tile(j, t):
+            source, dest, row0 = runs[j]
+            return dest[row0 : row0 + RUN * P, :].rearrange("(p t) f -> p t f", t=RUN)[:, t, :]
+
+        def prepare_weight(j):
+            quantize_weight(j, copy_out(transpose(w_rows[j]), j % VECTOR_COPY_EVERY == 1))
+
         w_tiles = F // P
-        w_rows = [load_weight(j) for j in range(w_tiles // 2)]
+        w_half = w_tiles // HALVES
+        w_rows = [load_weight(j) for j in range(w_half)]
         x_rows = [load_run(0)]
-        w_rows += [load_weight(j) for j in range(w_tiles // 2, w_tiles)]
+        w_rows += [load_weight(j) for j in range(w_half, w_tiles)]
         x_rows += [load_run(j) for j in range(1, len(runs))]
 
-        quantized = []
-        for j in range(w_tiles):
-            quantize_weight(j, copy_out(transpose(w_rows[j]), j % VECTOR_COPY_EVERY == 1))
-            if j == w_tiles // 2 - 1:
-                quantized = [quantize_rows(copy_out(transpose(rows), False)) for rows in x_rows[0]]
-
+        for j in range(w_half):
+            prepare_weight(j)
+        first = [quantize_rows(copy_out(transpose(rows), False)) for rows in x_rows[0]]
+        for j in range(w_half, w_half + RUN):
+            prepare_weight(j)
+        first_sums = [new_sums() for t in range(RUN)]
+        first_banks = [[multiply_half(first[t], 0, first_sums[t])] for t in range(RUN)]
+        for j in range(w_half + RUN, w_tiles):
+            prepare_weight(j)
+        quantized = [quantize_rows(copy_out(transpose(rows), False)) for rows in x_rows[1]]
         waiting = []
-        for j, (source, dest, row0, size) in enumerate(runs):
+        for t in range(RUN):
+            first_banks[t].append(multiply_half(first[t], 1, first_sums[t]))
+            waiting.append((first_banks[t], inverse_norm(first_sums[t]), dest_tile(0, t)))
+
+        for j in range(1, len(runs)):
             ahead = x_rows[j + 1] if j + 1 < len(runs) else []
             turned = [transpose(rows) for rows in ahead]
-            for item in waiting:
-                scale_and_store(*item)
-            waiting = []
-            grouped = [copy_out(bank, t == VECTOR_COPY_EVERY - 1) for t, bank in enumerate(turned)]
+            result_a, result_b = new_result(), new_result()
+            scale_half(waiting[0], 0, result_a)
+            scale_half(waiting[0], 1, result_a)
+            grouped = [
+                copy_out(bank, (RUN * j + t) % VECTOR_COPY_EVERY == VECTOR_COPY_EVERY - 1)
+                for t, bank in enumerate(turned)
+            ]
+            scale_half(waiting[1], 0, result_b)
             quantized_ahead = [quantize_rows(tile) for tile in grouped]
-            dest_tiles = dest[row0 : row0 + size * P, :].rearrange("(p t) f -> p t f", t=size)
-            for t in range(size):
-                banks, inverse = multiply(*quantized[t])
-                if t < size - LAG:
-                    scale_and_store(banks, inverse, dest_tiles[:, t, :])
-                else:
-                    waiting.append((banks, inverse, dest_tiles[:, t, :]))
+            scale_half(waiting[1], 1, result_b)
+            waiting = []
+            for t in range(RUN):
+                sums = new_sums()
+                banks = [multiply_half(quantized[t], h, sums) for h in range(HALVES)]
+                waiting.append((banks, inverse_norm(sums), dest_tile(j, t)))
             quantized = quantized_ahead
-        for item in waiting[:-1]:
-            scale_and_store(*item)
-        scale_and_store_last(*waiting[-1])
+        result_a = new_result()
+        scale_half(waiting[0], 0, result_a)
+        scale_half(waiting[0], 1, result_a)
+        scale_and_store_last(*waiting[1])

@@ -23,7 +23,7 @@ BANK = 512
 HALVES = F // BANK
 BANKS = 8
 RUN = 2
-VECTOR_COPY_EVERY = 3
+AHEAD = 2
 RESULT_BUFS = 16
 
 
@@ -69,26 +69,27 @@ def tile_minerva_old_pa_kernel(tc, features, ex_features, g_weight, out_0, out_1
             nc.sync.dma_start(out=rows[:], in_=source[row0 : row0 + RUN * P, :].rearrange("(p t) k -> p t k", t=RUN))
             return [rows[:, t, :] for t in range(RUN)]
 
-        def transpose(rows):
-            words = rows.bitcast(F32)
+        def sort_words(rows):
+            ordered = stage.tile([P, D], BF16, name="ordered", tag="ordered")
+            nc.vector.tensor_copy(
+                out=ordered[:].rearrange("p (u b i) -> p u b i", u=2, i=16),
+                in_=rows.rearrange("p (b u i) -> p u b i", u=2, i=16),
+            )
+            return ordered
+
+        def transpose(ordered):
+            words = ordered[:].bitcast(F32)
             number, bank = take_bank()
-            for g in range(PASSES):
-                for u in range(2):
-                    col = (2 * g + u) * P
-                    nc.tensor.transpose(
-                        bank[:, col : col + P], words[:, PASS_WORDS * g + u : PASS_WORDS * (g + 1) : 2], ident[:]
-                    )
+            for col in range(0, BANK, P):
+                nc.tensor.transpose(bank[:, col : col + P], words[:, col : col + P], ident[:])
             return number, bank
 
-        def copy_out(taken, on_vector):
+        def copy_out(taken):
             number, bank = taken
             grouped = stage.tile([P, BANK], F32, name="grouped", tag="grouped", align_bytes=64)
             dst = grouped[:].rearrange("p (g r u) -> p g r u", g=PASSES, u=2)
-            src = bank[:].rearrange("p (g u r) -> p g r u", g=PASSES, u=2)
-            if on_vector:
-                nc.vector.tensor_copy(out=dst, in_=src)
-            else:
-                nc.scalar.copy(out=dst, in_=src)
+            src = bank[:].rearrange("p (u g r) -> p g r u", g=PASSES, u=2)
+            nc.scalar.copy(out=dst, in_=src)
             free_banks.append(number)
             return grouped
 
@@ -107,7 +108,7 @@ def tile_minerva_old_pa_kernel(tc, features, ex_features, g_weight, out_0, out_1
             nc.vector.quantize_mx(out=x_codes[:].bitcast(E5M2), scales=x_scales[:], in_=grouped[:].bitcast(BF16))
             return x_codes, x_scales
 
-        def multiply_half(operand, h, sums):
+        def multiply_half(operand, h):
             x_codes, x_scales = operand
             number, bank = take_bank()
             cols = slice(h * BANK, (h + 1) * BANK)
@@ -121,9 +122,11 @@ def tile_minerva_old_pa_kernel(tc, features, ex_features, g_weight, out_0, out_1
                     start=(g == 0),
                     stop=(g == PASSES - 1),
                 )
-            squares = scratch.tile([P, BANK], F32, name="squares", tag="squares")
-            nc.scalar.activation(out=squares[:], in_=bank[:], func=ACT.Square, accum_out=sums[:, h : h + 1])
             return number, bank
+
+        def sum_squares(taken, h, sums):
+            squares = scratch.tile([P, BANK], F32, name="squares", tag="squares")
+            nc.scalar.activation(out=squares[:], in_=taken[1][:], func=ACT.Square, accum_out=sums[:, h : h + 1])
 
         def new_sums():
             sums = small.tile([P, HALVES], F32, name="sums", tag="sums")
@@ -164,9 +167,6 @@ def tile_minerva_old_pa_kernel(tc, features, ex_features, g_weight, out_0, out_1
             source, dest, row0 = runs[j]
             return dest[row0 : row0 + RUN * P, :].rearrange("(p t) f -> p t f", t=RUN)[:, t, :]
 
-        def prepare_weight(j):
-            quantize_weight(j, copy_out(transpose(w_rows[j]), j % VECTOR_COPY_EVERY == 1))
-
         w_tiles = F // P
         w_half = w_tiles // HALVES
         w_rows = [load_weight(j) for j in range(w_half)]
@@ -174,38 +174,53 @@ def tile_minerva_old_pa_kernel(tc, features, ex_features, g_weight, out_0, out_1
         w_rows += [load_weight(j) for j in range(w_half, w_tiles)]
         x_rows += [load_run(j) for j in range(1, len(runs))]
 
-        for j in range(w_half):
-            prepare_weight(j)
-        first = [quantize_rows(copy_out(transpose(rows), False)) for rows in x_rows[0]]
-        for j in range(w_half, w_half + RUN):
-            prepare_weight(j)
+        head = [(w_rows[j], j) for j in range(w_half)] + [(rows, None) for rows in x_rows[0]]
+        head += [(w_rows[j], j) for j in range(w_half, w_tiles)] + [(rows, None) for rows in x_rows[1]]
+        first_half_at = w_half + RUN - 1 + AHEAD
+        weights_turned_at = w_tiles + RUN - 1
+        head_grouped, head_quantized, ordered_ahead = [], [], []
         first_sums = [new_sums() for t in range(RUN)]
-        first_banks = [[multiply_half(first[t], 0, first_sums[t])] for t in range(RUN)]
-        for j in range(w_half + RUN, w_tiles):
-            prepare_weight(j)
-        quantized = [quantize_rows(copy_out(transpose(rows), False)) for rows in x_rows[1]]
+        first_banks = []
+        for i in range(len(head) + AHEAD):
+            if i < len(head):
+                head_grouped.append(copy_out(transpose(sort_words(head[i][0]))))
+            else:
+                ordered_ahead.append(sort_words(x_rows[2][i - len(head)]))
+            if i >= AHEAD:
+                weight_tile = head[i - AHEAD][1]
+                if weight_tile is None:
+                    head_quantized.append(quantize_rows(head_grouped[i - AHEAD]))
+                else:
+                    quantize_weight(weight_tile, head_grouped[i - AHEAD])
+            if i == first_half_at:
+                first_banks = [[multiply_half(head_quantized[t], 0)] for t in range(RUN)]
+            if i == weights_turned_at:
+                for t in range(RUN):
+                    sum_squares(first_banks[t][0], 0, first_sums[t])
         waiting = []
         for t in range(RUN):
-            first_banks[t].append(multiply_half(first[t], 1, first_sums[t]))
+            first_banks[t].append(multiply_half(head_quantized[t], 1))
+            sum_squares(first_banks[t][1], 1, first_sums[t])
             waiting.append((first_banks[t], inverse_norm(first_sums[t]), dest_tile(0, t)))
+        quantized = head_quantized[RUN:]
 
         for j in range(1, len(runs)):
-            ahead = x_rows[j + 1] if j + 1 < len(runs) else []
-            turned = [transpose(rows) for rows in ahead]
+            turned = [transpose(ordered) for ordered in ordered_ahead]
             result_a, result_b = new_result(), new_result()
             scale_half(waiting[0], 0, result_a)
             scale_half(waiting[0], 1, result_a)
-            grouped = [
-                copy_out(bank, (RUN * j + t) % VECTOR_COPY_EVERY == VECTOR_COPY_EVERY - 1)
-                for t, bank in enumerate(turned)
-            ]
-            scale_half(waiting[1], 0, result_b)
+            grouped = [copy_out(taken) for taken in turned]
+            ordered_ahead = [sort_words(rows) for rows in x_rows[j + 2]] if j + 2 < len(runs) else []
             quantized_ahead = [quantize_rows(tile) for tile in grouped]
+            scale_half(waiting[1], 0, result_b)
             scale_half(waiting[1], 1, result_b)
             waiting = []
             for t in range(RUN):
                 sums = new_sums()
-                banks = [multiply_half(quantized[t], h, sums) for h in range(HALVES)]
+                banks = []
+                for h in range(HALVES):
+                    banks.append(multiply_half(quantized[t], h))
+                    sum_squares(banks[h], h, sums)
                 waiting.append((banks, inverse_norm(sums), dest_tile(j, t)))
             quantized = quantized_ahead
         result_a = new_result()

@@ -23,7 +23,8 @@ BANK = 512
 HALVES = F // BANK
 BANKS = 8
 RUN = 2
-AHEAD = 2
+HEAD_VECTOR_COPY_EVERY = 3
+SORT_AHEAD = 3
 RESULT_BUFS = 16
 
 
@@ -70,28 +71,32 @@ def tile_minerva_old_pa_kernel(tc, features, ex_features, g_weight, out_0, out_1
             return [rows[:, t, :] for t in range(RUN)]
 
         def sort_words(rows):
-            ordered = stage.tile([P, D], BF16, name="ordered", tag="ordered")
-            nc.vector.tensor_copy(
-                out=ordered[:].rearrange("p (u b i) -> p u b i", u=2, i=16),
-                in_=rows.rearrange("p (b u i) -> p u b i", u=2, i=16),
-            )
-            return ordered
+            ordered = stage.tile([P, 2, PASSES * P], F32, name="ordered", tag="ordered")
+            nc.gpsimd.tensor_copy(out=ordered[:], in_=rows.bitcast(F32).rearrange("p (w u) -> p u w", u=2))
+            return ordered[:]
 
-        def transpose(ordered):
-            words = ordered[:].bitcast(F32)
+        def unsorted_words(rows):
+            return rows.bitcast(F32).rearrange("p (w u) -> p u w", u=2)
+
+        def transpose(words):
             number, bank = take_bank()
-            for col in range(0, BANK, P):
-                nc.tensor.transpose(bank[:, col : col + P], words[:, col : col + P], ident[:])
+            for g in range(PASSES):
+                for u in range(2):
+                    col = (2 * g + u) * P
+                    nc.tensor.transpose(bank[:, col : col + P], words[:, u, g * P : (g + 1) * P], ident[:])
             return number, bank
 
-        def copy_out(taken):
-            number, bank = taken
-            grouped = stage.tile([P, BANK], F32, name="grouped", tag="grouped", align_bytes=64)
-            dst = grouped[:].rearrange("p (g r u) -> p g r u", g=PASSES, u=2)
-            src = bank[:].rearrange("p (u g r) -> p g r u", g=PASSES, u=2)
-            nc.scalar.copy(out=dst, in_=src)
-            free_banks.append(number)
+        def new_grouped(tiles):
+            grouped = stage.tile([P, tiles * BANK], F32, name="grouped", tag="grouped", align_bytes=64)
             return grouped
+
+        def copy_out(src, dst, on_vector):
+            dst = dst.rearrange("p (g r u) -> p g r u", r=P, u=2)
+            src = src.rearrange("p (g u r) -> p g r u", r=P, u=2)
+            if on_vector:
+                nc.vector.tensor_copy(out=dst, in_=src)
+            else:
+                nc.scalar.copy(out=dst, in_=src)
 
         def quantize_weight(j, grouped):
             for g in range(PASSES):
@@ -102,11 +107,15 @@ def tile_minerva_old_pa_kernel(tc, features, ex_features, g_weight, out_0, out_1
                     in_=grouped[:, PASS_WORDS * g : PASS_WORDS * (g + 1)].bitcast(BF16),
                 )
 
-        def quantize_rows(grouped):
-            x_codes = stage.tile([P, PASSES * P], U32, name="x_codes", tag="x_codes", align_bytes=64)
-            x_scales = stage.tile([P, PASSES * P], U8, name="x_scales", tag="x_scales", align_bytes=64)
+        def quantize_rows(grouped, tiles):
+            width = PASSES * P
+            x_codes = stage.tile([P, tiles * width], U32, name="x_codes", tag="x_codes", align_bytes=64)
+            x_scales = stage.tile([P, tiles * width], U8, name="x_scales", tag="x_scales", align_bytes=64)
             nc.vector.quantize_mx(out=x_codes[:].bitcast(E5M2), scales=x_scales[:], in_=grouped[:].bitcast(BF16))
-            return x_codes, x_scales
+            return [
+                (x_codes[:, t * width : (t + 1) * width], x_scales[:, t * width : (t + 1) * width])
+                for t in range(tiles)
+            ]
 
         def multiply_half(operand, h):
             x_codes, x_scales = operand
@@ -176,42 +185,53 @@ def tile_minerva_old_pa_kernel(tc, features, ex_features, g_weight, out_0, out_1
 
         head = [(w_rows[j], j) for j in range(w_half)] + [(rows, None) for rows in x_rows[0]]
         head += [(w_rows[j], j) for j in range(w_half, w_tiles)] + [(rows, None) for rows in x_rows[1]]
-        first_half_at = w_half + RUN - 1 + AHEAD
+        first_half_at = w_half + 2 * RUN - 1
         weights_turned_at = w_tiles + RUN - 1
-        head_grouped, head_quantized, ordered_ahead = [], [], []
+        head_grouped, head_quantized = [], []
         first_sums = [new_sums() for t in range(RUN)]
         first_banks = []
-        for i in range(len(head) + AHEAD):
+        for i in range(len(head) + 1):
             if i < len(head):
-                head_grouped.append(copy_out(transpose(sort_words(head[i][0]))))
-            else:
-                ordered_ahead.append(sort_words(x_rows[2][i - len(head)]))
-            if i >= AHEAD:
-                weight_tile = head[i - AHEAD][1]
+                number, bank = transpose(unsorted_words(head[i][0]))
+            if i >= 1:
+                weight_tile = head[i - 1][1]
                 if weight_tile is None:
-                    head_quantized.append(quantize_rows(head_grouped[i - AHEAD]))
+                    head_quantized += quantize_rows(head_grouped[i - 1], 1)
                 else:
-                    quantize_weight(weight_tile, head_grouped[i - AHEAD])
+                    quantize_weight(weight_tile, head_grouped[i - 1])
+            if i < len(head):
+                head_grouped.append(new_grouped(1))
+                copy_out(bank[:], head_grouped[i][:], i % HEAD_VECTOR_COPY_EVERY == 1)
+                free_banks.append(number)
             if i == first_half_at:
                 first_banks = [[multiply_half(head_quantized[t], 0)] for t in range(RUN)]
             if i == weights_turned_at:
                 for t in range(RUN):
                     sum_squares(first_banks[t][0], 0, first_sums[t])
+        ordered = {j: sort_words(x_rows[j][0]) for j in range(2, SORT_AHEAD)}
         waiting = []
         for t in range(RUN):
             first_banks[t].append(multiply_half(head_quantized[t], 1))
             sum_squares(first_banks[t][1], 1, first_sums[t])
             waiting.append((first_banks[t], inverse_norm(first_sums[t]), dest_tile(0, t)))
+        ordered[SORT_AHEAD] = sort_words(x_rows[SORT_AHEAD][0])
         quantized = head_quantized[RUN:]
 
         for j in range(1, len(runs)):
-            turned = [transpose(ordered) for ordered in ordered_ahead]
+            more = j + 1 < len(runs)
+            if more:
+                number_a, bank_a = transpose(ordered[j + 1])
+                number_b, bank_b = transpose(unsorted_words(x_rows[j + 1][1]))
             result_a, result_b = new_result(), new_result()
             scale_half(waiting[0], 0, result_a)
             scale_half(waiting[0], 1, result_a)
-            grouped = [copy_out(taken) for taken in turned]
-            ordered_ahead = [sort_words(rows) for rows in x_rows[j + 2]] if j + 2 < len(runs) else []
-            quantized_ahead = [quantize_rows(tile) for tile in grouped]
+            if more:
+                grouped = new_grouped(RUN)
+                copy_out(bank_a[:], grouped[:, :BANK], False)
+                copy_out(bank_b[:, :PASS_WORDS], grouped[:, BANK : BANK + PASS_WORDS], False)
+                copy_out(bank_b[:, PASS_WORDS:], grouped[:, BANK + PASS_WORDS :], True)
+                free_banks.extend([number_a, number_b])
+                quantized_ahead = quantize_rows(grouped, RUN)
             scale_half(waiting[1], 0, result_b)
             scale_half(waiting[1], 1, result_b)
             waiting = []
@@ -222,6 +242,8 @@ def tile_minerva_old_pa_kernel(tc, features, ex_features, g_weight, out_0, out_1
                     banks.append(multiply_half(quantized[t], h))
                     sum_squares(banks[h], h, sums)
                 waiting.append((banks, inverse_norm(sums), dest_tile(j, t)))
+            if j + SORT_AHEAD < len(runs):
+                ordered[j + SORT_AHEAD] = sort_words(x_rows[j + SORT_AHEAD][0])
             quantized = quantized_ahead
         result_a = new_result()
         scale_half(waiting[0], 0, result_a)

from contextlib import ExitStack

import concourse.mybir as mybir
from concourse.masks import make_identity

B, N, D, F = 1024, 4096, 1024, 1024
EPS = 1e-12
FLOPS = 2 * (B + N) * D * F

F32 = mybir.dt.float32
BF16 = mybir.dt.bfloat16
U32 = mybir.dt.uint32
U8 = mybir.dt.uint8
E4M3 = mybir.dt.float8_e4m3fn_x4
E5M2 = mybir.dt.float8_e5m2_x4
ALU = mybir.AluOpType
ACT = mybir.ActivationFunctionType

P = 128
PASSES = D // 512
PASS_WORDS = 256
BANK = 512
HALVES = F // BANK
BANKS = 8
RUN = 2
HEAD_VECTOR_COPY_EVERY = 3
SORT_AHEAD = 3
RESULT_BUFS = 16


def tile_minerva_old_pa_kernel(tc, features, ex_features, g_weight, out_0, out_1):
    nc = tc.nc

    runs = [(features, out_0, row) for row in range(0, B, RUN * P)]
    runs += [(ex_features, out_1, row) for row in range(0, N, RUN * P)]

    with ExitStack() as ctx:
        keep = ctx.enter_context(tc.tile_pool(name="keep", bufs=1))
        stage = ctx.enter_context(tc.tile_pool(name="stage", bufs=3 * RUN))
        small = ctx.enter_context(tc.tile_pool(name="small", bufs=3 * RUN))
        results = ctx.enter_context(tc.tile_pool(name="results", bufs=RESULT_BUFS))
        scratch = ctx.enter_context(tc.tile_pool(name="scratch", bufs=2))
        psum = ctx.enter_context(tc.psum_pool(name="psum", bufs=1))
        ctx.enter_context(tc.manual_schedule())

        ident = keep.tile([P, P], F32)
        make_identity(nc, ident[:])
        minus_half = keep.tile([P, 1], F32)
        nc.gpsimd.memset(minus_half[:], -0.5)

        w_codes = keep.tile([P, PASSES, F], U32, align_bytes=64)
        w_scales = keep.tile([P, PASSES, F], U8, align_bytes=64)

        free_banks = list(range(BANKS))

        def take_bank():
            number = free_banks[0]
            free_banks.remove(number)
            bank = psum.tile([P, BANK], F32, name="bank%d" % number, tag="bank%d" % number)
            return number, bank

        def load_weight(j):
            rows = keep.tile([P, D], BF16, name="w_rows%d" % j, tag="w_rows%d" % j)
            nc.sync.dma_start(out=rows[:], in_=g_weight[j * P : (j + 1) * P, :])
            return rows[:]

        def load_run(j):
            source, dest, row0 = runs[j]
            rows = keep.tile([P, RUN, D], BF16, name="x_rows%d" % j, tag="x_rows%d" % j)
            nc.sync.dma_start(out=rows[:], in_=source[row0 : row0 + RUN * P, :].rearrange("(p t) k -> p t k", t=RUN))
            return [rows[:, t, :] for t in range(RUN)]

        def sort_words(rows):
            ordered = stage.tile([P, 2, PASSES * P], F32, name="ordered", tag="ordered")
            nc.gpsimd.tensor_copy(out=ordered[:], in_=rows.bitcast(F32).rearrange("p (w u) -> p u w", u=2))
            return ordered[:]

        def unsorted_words(rows):
            return rows.bitcast(F32).rearrange("p (w u) -> p u w", u=2)

        def transpose(words):
            number, bank = take_bank()
            for g in range(PASSES):
                for u in range(2):
                    col = (2 * g + u) * P
                    nc.tensor.transpose(bank[:, col : col + P], words[:, u, g * P : (g + 1) * P], ident[:])
            return number, bank

        def new_grouped(tiles):
            grouped = stage.tile([P, tiles * BANK], F32, name="grouped", tag="grouped", align_bytes=64)
            return grouped

        def copy_out(src, dst, on_vector):
            dst = dst.rearrange("p (g r u) -> p g r u", r=P, u=2)
            src = src.rearrange("p (g u r) -> p g r u", r=P, u=2)
            if on_vector:
                nc.vector.tensor_copy(out=dst, in_=src)
            else:
                nc.scalar.copy(out=dst, in_=src)

        def quantize_weight(j, grouped):
            for g in range(PASSES):
                cols = slice(j * P, (j + 1) * P)
                nc.vector.quantize_mx(
                    out=w_codes[:, g, cols].bitcast(E4M3),
                    scales=w_scales[:, g, cols],
                    in_=grouped[:, PASS_WORDS * g : PASS_WORDS * (g + 1)].bitcast(BF16),
                )

        def quantize_rows(grouped, tiles):
            width = PASSES * P
            x_codes = stage.tile([P, tiles * width], U32, name="x_codes", tag="x_codes", align_bytes=64)
            x_scales = stage.tile([P, tiles * width], U8, name="x_scales", tag="x_scales", align_bytes=64)
            nc.vector.quantize_mx(out=x_codes[:].bitcast(E5M2), scales=x_scales[:], in_=grouped[:].bitcast(BF16))
            return [
                (x_codes[:, t * width : (t + 1) * width], x_scales[:, t * width : (t + 1) * width])
                for t in range(tiles)
            ]

        def multiply_half(operand, h):
            x_codes, x_scales = operand
            number, bank = take_bank()
            cols = slice(h * BANK, (h + 1) * BANK)
            for g in range(PASSES):
                nc.tensor.matmul_mx(
                    out=bank[:],
                    lhsT=x_codes[:, g * P : (g + 1) * P].bitcast(E5M2),
                    lhsT_scale=x_scales[:, g * P : (g + 1) * P],
                    rhs=w_codes[:, g, cols].bitcast(E4M3),
                    rhs_scale=w_scales[:, g, cols],
                    start=(g == 0),
                    stop=(g == PASSES - 1),
                )
            return number, bank

        def sum_squares(taken, h, sums):
            squares = scratch.tile([P, BANK], F32, name="squares", tag="squares")
            nc.scalar.activation(out=squares[:], in_=taken[1][:], func=ACT.Square, accum_out=sums[:, h : h + 1])

        def new_sums():
            sums = small.tile([P, HALVES], F32, name="sums", tag="sums")
            return sums

        def inverse_norm(sums):
            floored = small.tile([P, 1], F32, name="floored", tag="floored")
            nc.gpsimd.tensor_scalar(
                out=floored[:], in0=sums[:, 0:1], scalar1=sums[:, 1:2], scalar2=EPS * EPS, op0=ALU.add, op1=ALU.max
            )
            inverse = small.tile([P, 1], F32, name="inverse", tag="inverse")
            nc.gpsimd.tensor_tensor(out=inverse[:], in0=floored[:], in1=minus_half[:], op=ALU.pow)
            return inverse

        def new_result():
            result = results.tile([P, F], F32, name="result", tag="result")
            return result

        def scale_half(item, h, result):
            banks, inverse, dest_rows = item
            number, bank = banks[h]
            nc.vector.tensor_scalar(
                out=result[:, h * BANK : (h + 1) * BANK], in0=bank[:], scalar1=inverse[:], scalar2=None, op0=ALU.mult
            )
            free_banks.append(number)
            if h == HALVES - 1:
                nc.sync.dma_start(out=dest_rows, in_=result[:])

        def scale_and_store_last(banks, inverse, dest_rows):
            result = results.tile([P, F], F32, name="result", tag="result")
            nc.vector.tensor_scalar(
                out=result[:, :BANK], in0=banks[0][1][:], scalar1=inverse[:], scalar2=None, op0=ALU.mult
            )
            nc.scalar.activation(out=result[:, BANK:], in_=banks[1][1][:], func=ACT.Copy, scale=inverse[:])
            nc.sync.dma_start(out=dest_rows, in_=result[:])

        def dest_tile(j, t):
            source, dest, row0 = runs[j]
            return dest[row0 : row0 + RUN * P, :].rearrange("(p t) f -> p t f", t=RUN)[:, t, :]

        w_tiles = F // P
        w_half = w_tiles // HALVES
        w_rows = [load_weight(j) for j in range(w_half)]
        x_rows = [load_run(0)]
        w_rows += [load_weight(j) for j in range(w_half, w_tiles)]
        x_rows += [load_run(j) for j in range(1, len(runs))]

        head = [(w_rows[j], j) for j in range(w_half)] + [(rows, None) for rows in x_rows[0]]
        head += [(w_rows[j], j) for j in range(w_half, w_tiles)] + [(rows, None) for rows in x_rows[1]]
        first_half_at = w_half + 2 * RUN - 1
        weights_turned_at = w_tiles + RUN - 1
        head_grouped, head_quantized = [], []
        first_sums = [new_sums() for t in range(RUN)]
        first_banks = []
        for i in range(len(head) + 1):
            if i < len(head):
                number, bank = transpose(unsorted_words(head[i][0]))
            if i >= 1:
                weight_tile = head[i - 1][1]
                if weight_tile is None:
                    head_quantized += quantize_rows(head_grouped[i - 1], 1)
                else:
                    quantize_weight(weight_tile, head_grouped[i - 1])
            if i < len(head):
                head_grouped.append(new_grouped(1))
                copy_out(bank[:], head_grouped[i][:], i % HEAD_VECTOR_COPY_EVERY == 1)
                free_banks.append(number)
            if i == first_half_at:
                first_banks = [[multiply_half(head_quantized[t], 0)] for t in range(RUN)]
            if i == weights_turned_at:
                for t in range(RUN):
                    sum_squares(first_banks[t][0], 0, first_sums[t])
        ordered = {j: sort_words(x_rows[j][0]) for j in range(2, SORT_AHEAD)}
        waiting = []
        for t in range(RUN):
            first_banks[t].append(multiply_half(head_quantized[t], 1))
            sum_squares(first_banks[t][1], 1, first_sums[t])
            waiting.append((first_banks[t], inverse_norm(first_sums[t]), dest_tile(0, t)))
        ordered[SORT_AHEAD] = sort_words(x_rows[SORT_AHEAD][0])
        quantized = head_quantized[RUN:]

        for j in range(1, len(runs)):
            more = j + 1 < len(runs)
            if more:
                number_a, bank_a = transpose(ordered[j + 1])
                number_b, bank_b = transpose(unsorted_words(x_rows[j + 1][1]))
            result_a, result_b = new_result(), new_result()
            scale_half(waiting[0], 0, result_a)
            scale_half(waiting[0], 1, result_a)
            if more:
                grouped = new_grouped(RUN)
                copy_out(bank_a[:], grouped[:, :BANK], False)
                copy_out(bank_b[:, :PASS_WORDS], grouped[:, BANK : BANK + PASS_WORDS], False)
                copy_out(bank_b[:, PASS_WORDS:], grouped[:, BANK + PASS_WORDS :], True)
                free_banks.extend([number_a, number_b])
                quantized_ahead = quantize_rows(grouped, RUN)
            scale_half(waiting[1], 0, result_b)
            scale_half(waiting[1], 1, result_b)
            waiting = []
            for t in range(RUN):
                sums = new_sums()
                banks = []
                for h in range(HALVES):
                    banks.append(multiply_half(quantized[t], h))
                    sum_squares(banks[h], h, sums)
                waiting.append((banks, inverse_norm(sums), dest_tile(j, t)))
            if j + SORT_AHEAD < len(runs):
                ordered[j + SORT_AHEAD] = sort_words(x_rows[j + SORT_AHEAD][0])
            quantized = quantized_ahead
        result_a = new_result()
        scale_half(waiting[0], 0, result_a)
        scale_half(waiting[0], 1, result_a)
        scale_and_store_last(*waiting[1])
